import numpy as np
import ml_dtypes


def mxq(x, axis, fmt="e4m3"):
    dtype, down = {"e4m3": (ml_dtypes.float8_e4m3fn, 7), "e5m2": (ml_dtypes.float8_e5m2, 14)}[fmt]
    v = np.moveaxis(np.asarray(x, np.float32).astype(ml_dtypes.bfloat16).astype(np.float64), axis, -1)
    blocks = v.reshape(v.shape[:-1] + (-1, 32))
    amax = np.abs(blocks).max(-1, keepdims=True)
    byte = np.maximum(np.where(amax > 0, np.frexp(amax)[1] - 1 + 127, 0) - down, 1)
    scale = np.exp2(byte - 127.0)
    codes = (blocks / scale).astype(np.float32).astype(dtype).astype(np.float64)
    return np.moveaxis((codes * scale).reshape(v.shape), -1, axis)


WIDE = False


def mx_kscale(k):
    if not WIDE:
        return np.ones(k)
    levels = np.array([10, -10, 5, -5, 0])
    a = np.random.permutation(np.resize(levels, k // 512 * 4)).reshape(k // 512, 4)
    idx = np.arange(k)
    return np.exp2(a[idx // 512, idx % 128 // 32])


BF16 = ml_dtypes.bfloat16


def bf(x):
    return np.asarray(x, np.float32).astype(BF16)


def f64(x):
    return np.asarray(x).astype(np.float64)


E2M1 = np.array([0.0, 0.5, 1.0, 1.5, 2.0, 3.0, 4.0, 6.0, -0.0, -0.5, -1.0, -1.5, -2.0, -3.0, -4.0, -6.0])


def pack_weight(w, fmt):
    k, n = w.shape
    w = f64(bf(w)).reshape(k // 32, 32, n)
    amax = np.abs(w).max(1)
    if fmt == "e4m3":
        byte = np.frexp(amax)[1] - 1 + 127 - 7
    else:
        mant, ex = np.frexp(amax / 6.0)
        byte = np.where(mant > 0.5, ex, ex - 1) + 127
    byte = np.clip(np.where(amax > 0, byte, 1), 1, 254)
    scaled = (w * np.exp2(127.0 - byte)[:, None, :]).reshape(k, n).astype(np.float32)
    by_word = np.ascontiguousarray(scaled.reshape(k // 512, 128, 4, n).transpose(0, 1, 3, 2))
    if fmt == "e4m3":
        words = by_word.astype(ml_dtypes.float8_e4m3fn).view(np.uint8)
    else:
        c = by_word.astype(ml_dtypes.float4_e2m1fn).view(np.uint8) & 0xF
        words = c[..., 0::2] | (c[..., 1::2] << 4)
    return np.ascontiguousarray(words), np.ascontiguousarray(byte.astype(np.uint8).reshape(k // 512, 16, n))


def unpack_weight(words, scales, fmt):
    g, p, n, _ = words.shape
    if fmt == "e4m3":
        vals = np.ascontiguousarray(words).view(ml_dtypes.float8_e4m3fn).astype(np.float64)
    else:
        nib = np.empty((g, p, n, 4), np.uint8)
        nib[..., 0::2] = words & 0xF
        nib[..., 1::2] = words >> 4
        vals = E2M1[nib]
    vals = vals * np.repeat(np.exp2(scales.astype(np.float64) - 127.0), 8, axis=1)[..., None]
    return vals.transpose(0, 1, 3, 2).reshape(g * 512, n)


B, C, H, W, O, KH, KW, PH, PW, T, R = 4, 256, 31, 32, 256, 2, 1, 1, 0, 8, 64
HO, WO = H + PH + PH - KH + 1, W + PW + PW - KW + 1
N = B * HO * WO
D = C * KH * KW
R2 = R * KH * KW
K1, K2 = T * R, T * R2
FMT = "e4m3"


def setup_inputs():
    s, t1, t2 = mx_kscale(D), mx_kscale(K1).reshape(T, R), mx_kscale(K2).reshape(T, R2)
    xw = bf(np.random.standard_normal((N, D)) * s)
    s1_stack = np.random.standard_normal((T, D, R)) / np.sqrt(D) / s[None, :, None] * t1[:, None, :]
    S1s_words, S1s_scales = pack_weight(s1_stack.reshape(-1, R), FMT)
    U1s = bf(np.random.standard_normal((T, R, O)) * T / np.sqrt(K1) / t1[:, :, None])
    u2_stack = np.random.standard_normal((T, R2, D)) / np.sqrt(D) / s[None, None, :] * t2[:, :, None]
    U2s_words, U2s_scales = pack_weight(u2_stack.swapaxes(1, 2).reshape(-1, R2), FMT)
    S2s = bf(np.random.standard_normal((T, R2, O)) * T / np.sqrt(K2) / t2[:, :, None])
    bias = bf(np.random.standard_normal(O) * 0.3)
    return {"xw": xw,
            "S1s_words": S1s_words, "S1s_scales": S1s_scales,
            "U1s": U1s,
            "U2s_words": U2s_words, "U2s_scales": U2s_scales,
            "S2s": S2s,
            "bias": bias}


def reference(xw, S1s_words, S1s_scales, U1s, U2s_words, U2s_scales, S2s, bias):
    xq = mxq(f64(xw), 1, "e4m3")
    s1 = unpack_weight(S1s_words, S1s_scales, FMT).reshape(T, D, R).transpose(1, 0, 2).reshape(D, K1)
    h1 = xq @ s1
    out1 = (mxq(h1, 1, "e4m3") @ mxq(f64(U1s).reshape(K1, O), 0, "e4m3")) / T + f64(bias)
    u2t = unpack_weight(U2s_words, U2s_scales, FMT).reshape(T, D, R2).transpose(1, 0, 2).reshape(D, K2)
    h2 = xq @ u2t
    out2 = (mxq(h2, 1, "e4m3") @ mxq(f64(S2s).reshape(K2, O), 0, "e4m3")) / T
    out = out1 + out2 + f64(bias)
    return out.reshape(B, HO, WO, O).transpose(0, 3, 1, 2)

@@ -1,0 +1,231 @@
+from contextlib import ExitStack
+
+import concourse.mybir as mybir
+from concourse.masks import make_identity
+
+F32 = mybir.dt.float32
+BF16 = mybir.dt.bfloat16
+I32 = mybir.dt.int32
+U32 = mybir.dt.uint32
+U8 = mybir.dt.uint8
+FP8X4 = mybir.dt.float8_e4m3fn_x4
+IDENTITY = mybir.ActivationFunctionType.Identity
+
+P = 128
+PACK = 4
+K_PASS = P * PACK
+
+WINDOWS = 4096
+D = 512
+TERMS = 8
+H1 = 512
+HIDDEN = 1536
+HIDDEN_PASSES = HIDDEN // K_PASS
+OUT_CH = 256
+OUT_TILES = OUT_CH // P
+IMAGE = 1024
+
+GROUP = 512
+GROUPS = WINDOWS // GROUP
+PIECE = 128
+PIECES = GROUP // PIECE
+SCALE_ROWS = 4
+QUADRANTS = 4
+
+FLOPS = 2 * WINDOWS * D * HIDDEN + 2 * WINDOWS * HIDDEN * OUT_CH
+
+
+def tile_skconv2d_pa_t_e_kernel(
+    tc, xw, S1s_words, S1s_scales, U1s, U2s_words, U2s_scales, S2s, bias, out
+):
+    nc = tc.nc
+    with ExitStack() as ctx:
+        const = ctx.enter_context(tc.tile_pool(name="const", bufs=1))
+        x_pool = ctx.enter_context(tc.tile_pool(name="x_rows", bufs=GROUPS))
+        pair = ctx.enter_context(tc.tile_pool(name="pair", bufs=2))
+        hg_pool = ctx.enter_context(tc.tile_pool(name="h_grouped", bufs=3))
+        y_pool = ctx.enter_context(tc.tile_pool(name="y", bufs=4))
+        xt_psum = ctx.enter_context(tc.psum_pool(name="xt_psum", bufs=2))
+        h_psum = ctx.enter_context(tc.psum_pool(name="h_psum", bufs=4))
+        y_psum = ctx.enter_context(tc.psum_pool(name="y_psum", bufs=2))
+        ctx.enter_context(tc.manual_schedule())
+
+        ident = const.tile([P, P], F32)
+        make_identity(nc, ident[:])
+
+        w1_words = const.tile([P, HIDDEN], U32, align_bytes=64)
+        w1_scales = const.tile([P, HIDDEN], U8, align_bytes=64)
+        nc.vector.memset(w1_scales[:].bitcast(I32), 0)
+
+        bias_cols = const.tile([P, OUT_TILES], BF16)
+        with nc.allow_non_contiguous_dma(reason="256 bias values, one per partition and tile"):
+            nc.sync.dma_start(out=bias_cols[:], in_=bias.rearrange("(t p) -> p t", p=P))
+
+        x_rows = {}
+
+        def load_x(g):
+            rows = x_pool.tile([P, PIECES, D], BF16, name="x_rows")
+            nc.sync.dma_start(
+                out=rows[:],
+                in_=xw[GROUP * g : GROUP * (g + 1), :].rearrange("(s p) d -> p s d", p=P),
+            )
+            x_rows[g] = rows
+
+        def load_stage1_weights(words, scales, first, count):
+            cols = slice(first, first + count)
+            nc.sync.dma_start(
+                out=w1_words[:, cols].bitcast(I32).rearrange("p (g n) -> p g n", g=TERMS),
+                in_=words.rearrange("g p n t -> p g (n t)").bitcast(I32),
+            )
+            for quadrant in range(QUADRANTS):
+                nc.sync.dma_start(
+                    out=w1_scales[32 * quadrant : 32 * quadrant + SCALE_ROWS, cols]
+                    .bitcast(I32)
+                    .rearrange("r (g n) -> r g n", g=TERMS),
+                    in_=scales[:, SCALE_ROWS * quadrant : SCALE_ROWS * (quadrant + 1), :]
+                    .rearrange("g r n -> r g n")
+                    .bitcast(I32),
+                )
+
+        w2_raw = const.tile([P, HIDDEN // P, OUT_CH], BF16)
+
+        load_x(0)
+        load_stage1_weights(S1s_words, S1s_scales, 0, H1)
+        load_x(1)
+        load_stage1_weights(U2s_words, U2s_scales, H1, HIDDEN - H1)
+        nc.sync.dma_start(
+            out=w2_raw[:, 0 : H1 // P, :],
+            in_=U1s.rearrange("t r o -> (t r) o").rearrange("(m p) o -> p m o", p=P),
+        )
+        nc.sync.dma_start(
+            out=w2_raw[:, H1 // P :, :],
+            in_=S2s.rearrange("t r o -> (t r) o").rearrange("(m p) o -> p m o", p=P),
+        )
+        for g in range(2, GROUPS):
+            load_x(g)
+
+        bias2 = const.tile([P, OUT_TILES], F32)
+        nc.scalar.activation(out=bias2[:], in_=bias_cols[:], func=IDENTITY, scale=2.0)
+
+        w2_grouped = const.tile([P, HIDDEN_PASSES, OUT_CH, PACK], BF16, align_bytes=64)
+        w2_words = const.tile([P, HIDDEN_PASSES, OUT_CH], U32, align_bytes=64)
+        w2_scales = const.tile([P, HIDDEN_PASSES, OUT_CH], U8, align_bytes=64)
+
+        def quantise_stage2_weights():
+            for c in range(HIDDEN_PASSES):
+                nc.vector.tensor_copy(
+                    out=w2_grouped[:, c],
+                    in_=w2_raw[:, PACK * c : PACK * (c + 1), :].rearrange("p j o -> p o j"),
+                )
+            for c in range(HIDDEN_PASSES):
+                nc.vector.quantize_mx(
+                    out=w2_words[:, c, :].bitcast(FP8X4),
+                    scales=w2_scales[:, c, :],
+                    in_=w2_grouped[:, c].rearrange("p o j -> p (o j)"),
+                )
+
+        x_grouped = {}
+        x_words = {}
+        x_scales = {}
+        h_grouped = {}
+        h_words = {}
+        h_scales = {}
+
+        def transpose_x(g):
+            grouped = pair.tile([P, GROUP * PACK], BF16, align_bytes=64, name="x_grouped")
+            grouped_words = grouped[:].bitcast(F32).rearrange("p (w u) -> p w u", u=2)
+            for half in range(2):
+                xt = xt_psum.tile([P, 2, 2 * PIECE], F32, name="xt")
+                for s in range(2):
+                    words = x_rows[g][:, 2 * half + s, :].bitcast(F32)
+                    for u in range(2):
+                        nc.tensor.transpose(
+                            xt[:, u, PIECE * s : PIECE * (s + 1)], words[:, u : D // 2 : 2], ident[:]
+                        )
+                nc.scalar.copy(
+                    out=grouped_words[:, 2 * PIECE * half : 2 * PIECE * (half + 1), :],
+                    in_=xt[:].rearrange("p u w -> p w u"),
+                )
+            x_grouped[g] = grouped
+
+        def quantise_x(g):
+            words = pair.tile([P, GROUP], U32, align_bytes=64, name="x_words")
+            scales = pair.tile([P, GROUP], U8, align_bytes=64, name="x_scales")
+            nc.vector.quantize_mx(out=words[:].bitcast(FP8X4), scales=scales[:], in_=x_grouped[g][:])
+            x_words[g] = words
+            x_scales[g] = scales
+
+        def stage1(g, c):
+            grouped = hg_pool.tile([P, GROUP, PACK], BF16, align_bytes=64, name="h_grouped")
+            for q in range(PIECES):
+                windows = slice(PIECE * q, PIECE * (q + 1))
+                h_bank = h_psum.tile([P, PACK, PIECE], F32, name="h_bank")
+                for j in range(PACK):
+                    rows = slice(K_PASS * c + P * j, K_PASS * c + P * (j + 1))
+                    nc.tensor.matmul_mx(
+                        out=h_bank[:, j, :],
+                        lhsT=w1_words[:, rows].bitcast(FP8X4),
+                        lhsT_scale=w1_scales[:, rows],
+                        rhs=x_words[g][:, windows].bitcast(FP8X4),
+                        rhs_scale=x_scales[g][:, windows],
+                        start=True,
+                        stop=True,
+                    )
+                copy = nc.scalar.copy if q % 2 == 0 else nc.vector.tensor_copy
+                copy(out=grouped[:, windows, :], in_=h_bank[:].rearrange("p j w -> p w j"))
+            h_grouped[(g, c)] = grouped
+
+        def quantise_h(g, c):
+            if c == 0:
+                words = pair.tile([P, HIDDEN_PASSES, GROUP], U32, align_bytes=64, name="h_words")
+                scales = pair.tile([P, HIDDEN_PASSES, GROUP], U8, align_bytes=64, name="h_scales")
+                h_words[g] = words
+                h_scales[g] = scales
+            nc.vector.quantize_mx(
+                out=h_words[g][:, c, :].bitcast(FP8X4),
+                scales=h_scales[g][:, c, :],
+                in_=h_grouped[(g, c)][:].rearrange("p w j -> p (w j)"),
+            )
+
+        out_rows = out.rearrange("b o i j -> b o (i j)")
+
+        def stage2(g):
+            image = GROUP * g // IMAGE
+            first = GROUP * g % IMAGE
+            for t in range(OUT_TILES):
+                channels = slice(P * t, P * (t + 1))
+                y_bank = y_psum.tile([P, GROUP], F32, name="y_bank")
+                for c in range(HIDDEN_PASSES):
+                    nc.tensor.matmul_mx(
+                        out=y_bank[:],
+                        lhsT=w2_words[:, c, channels].bitcast(FP8X4),
+                        lhsT_scale=w2_scales[:, c, channels],
+                        rhs=h_words[g][:, c, :].bitcast(FP8X4),
+                        rhs_scale=h_scales[g][:, c, :],
+                        start=(c == 0),
+                        stop=(c == HIDDEN_PASSES - 1),
+                    )
+                y_sb = y_pool.tile([P, GROUP], F32, name="y_sb")
+                nc.scalar.activation(
+                    out=y_sb[:], in_=y_bank[:], func=IDENTITY, bias=bias2[:, t : t + 1], scale=1.0 / TERMS
+                )
+                nc.sync.dma_start(out=out_rows[image, channels, first : first + GROUP], in_=y_sb[:])
+
+        transpose_x(0)
+        quantise_x(0)
+        for g in range(GROUPS):
+            stage1(g, 0)
+            if g + 1 < GROUPS:
+                transpose_x(g + 1)
+            stage1(g, 1)
+            quantise_h(g, 0)
+            if g + 1 < GROUPS:
+                quantise_x(g + 1)
+            stage1(g, 2)
+            quantise_h(g, 1)
+            if g == 0:
+                quantise_stage2_weights()
+            else:
+                stage2(g - 1)
+            quantise_h(g, 2)
+        stage2(GROUPS - 1)

@@ -29,6 +29,8 @@ GROUP = 512
 GROUPS = WINDOWS // GROUP
 PIECE = 128
 PIECES = GROUP // PIECE
+HALVES = 2
+HALF = GROUP // HALVES
 SCALE_ROWS = 4
 QUADRANTS = 4
 
@@ -41,7 +43,7 @@ def tile_skconv2d_pa_t_e_kernel(
     nc = tc.nc
     with ExitStack() as ctx:
         const = ctx.enter_context(tc.tile_pool(name="const", bufs=1))
-        x_pool = ctx.enter_context(tc.tile_pool(name="x_rows", bufs=GROUPS))
+        x_pool = ctx.enter_context(tc.tile_pool(name="x_rows", bufs=GROUPS * HALVES))
         pair = ctx.enter_context(tc.tile_pool(name="pair", bufs=2))
         hg_pool = ctx.enter_context(tc.tile_pool(name="h_grouped", bufs=3))
         y_pool = ctx.enter_context(tc.tile_pool(name="y", bufs=4))
@@ -64,12 +66,13 @@ def tile_skconv2d_pa_t_e_kernel(
         x_rows = {}
 
         def load_x(g):
-            rows = x_pool.tile([P, PIECES, D], BF16, name="x_rows")
-            nc.sync.dma_start(
-                out=rows[:],
-                in_=xw[GROUP * g : GROUP * (g + 1), :].rearrange("(s p) d -> p s d", p=P),
-            )
-            x_rows[g] = rows
+            for half in range(HALVES):
+                first = GROUP * g + HALF * half
+                rows = x_pool.tile([P, HALF // P, D], BF16, name="x_rows")
+                nc.sync.dma_start(
+                    out=rows[:], in_=xw[first : first + HALF, :].rearrange("(s p) d -> p s d", p=P)
+                )
+                x_rows[(g, half)] = rows
 
         def load_stage1_weights(words, scales, first, count):
             cols = slice(first, first + count)
@@ -113,7 +116,8 @@ def tile_skconv2d_pa_t_e_kernel(
 
         def quantise_stage2_weights():
             for c in range(HIDDEN_PASSES):
-                nc.vector.tensor_copy(
+                copy = nc.scalar.copy if c < HIDDEN_PASSES - 1 else nc.vector.tensor_copy
+                copy(
                     out=w2_grouped[:, c],
                     in_=w2_raw[:, PACK * c : PACK * (c + 1), :].rearrange("p j o -> p o j"),
                 )
@@ -134,16 +138,16 @@ def tile_skconv2d_pa_t_e_kernel(
         def transpose_x(g):
             grouped = pair.tile([P, GROUP * PACK], BF16, align_bytes=64, name="x_grouped")
             grouped_words = grouped[:].bitcast(F32).rearrange("p (w u) -> p w u", u=2)
-            for half in range(2):
-                xt = xt_psum.tile([P, 2, 2 * PIECE], F32, name="xt")
-                for s in range(2):
-                    words = x_rows[g][:, 2 * half + s, :].bitcast(F32)
+            for half in range(HALVES):
+                xt = xt_psum.tile([P, 2, HALF], F32, name="xt")
+                for s in range(HALF // P):
+                    words = x_rows[(g, half)][:, s, :].bitcast(F32)
                     for u in range(2):
                         nc.tensor.transpose(
-                            xt[:, u, PIECE * s : PIECE * (s + 1)], words[:, u : D // 2 : 2], ident[:]
+                            xt[:, u, P * s : P * (s + 1)], words[:, u : D // 2 : 2], ident[:]
                         )
                 nc.scalar.copy(
-                    out=grouped_words[:, 2 * PIECE * half : 2 * PIECE * (half + 1), :],
+                    out=grouped_words[:, HALF * half : HALF * (half + 1), :],
                     in_=xt[:].rearrange("p u w -> p w u"),
                 )
             x_grouped[g] = grouped
@@ -151,7 +155,13 @@ def tile_skconv2d_pa_t_e_kernel(
         def quantise_x(g):
             words = pair.tile([P, GROUP], U32, align_bytes=64, name="x_words")
             scales = pair.tile([P, GROUP], U8, align_bytes=64, name="x_scales")
-            nc.vector.quantize_mx(out=words[:].bitcast(FP8X4), scales=scales[:], in_=x_grouped[g][:])
+            for half in range(HALVES):
+                windows = slice(HALF * half, HALF * (half + 1))
+                nc.vector.quantize_mx(
+                    out=words[:, windows].bitcast(FP8X4),
+                    scales=scales[:, windows],
+                    in_=x_grouped[g][:, PACK * HALF * half : PACK * HALF * (half + 1)],
+                )
             x_words[g] = words
             x_scales[g] = scales
 
@@ -189,43 +199,47 @@ def tile_skconv2d_pa_t_e_kernel(
 
         out_rows = out.rearrange("b o i j -> b o (i j)")
 
-        def stage2(g):
+        def stage2(g, t):
             image = GROUP * g // IMAGE
             first = GROUP * g % IMAGE
-            for t in range(OUT_TILES):
-                channels = slice(P * t, P * (t + 1))
-                y_bank = y_psum.tile([P, GROUP], F32, name="y_bank")
-                for c in range(HIDDEN_PASSES):
-                    nc.tensor.matmul_mx(
-                        out=y_bank[:],
-                        lhsT=w2_words[:, c, channels].bitcast(FP8X4),
-                        lhsT_scale=w2_scales[:, c, channels],
-                        rhs=h_words[g][:, c, :].bitcast(FP8X4),
-                        rhs_scale=h_scales[g][:, c, :],
-                        start=(c == 0),
-                        stop=(c == HIDDEN_PASSES - 1),
-                    )
-                y_sb = y_pool.tile([P, GROUP], F32, name="y_sb")
-                nc.scalar.activation(
-                    out=y_sb[:], in_=y_bank[:], func=IDENTITY, bias=bias2[:, t : t + 1], scale=1.0 / TERMS
+            channels = slice(P * t, P * (t + 1))
+            y_bank = y_psum.tile([P, GROUP], F32, name="y_bank")
+            for c in range(HIDDEN_PASSES):
+                nc.tensor.matmul_mx(
+                    out=y_bank[:],
+                    lhsT=w2_words[:, c, channels].bitcast(FP8X4),
+                    lhsT_scale=w2_scales[:, c, channels],
+                    rhs=h_words[g][:, c, :].bitcast(FP8X4),
+                    rhs_scale=h_scales[g][:, c, :],
+                    start=(c == 0),
+                    stop=(c == HIDDEN_PASSES - 1),
                 )
-                nc.sync.dma_start(out=out_rows[image, channels, first : first + GROUP], in_=y_sb[:])
+            y_sb = y_pool.tile([P, GROUP], F32, name="y_sb")
+            nc.scalar.activation(
+                out=y_sb[:], in_=y_bank[:], func=IDENTITY, bias=bias2[:, t : t + 1], scale=1.0 / TERMS
+            )
+            nc.sync.dma_start(out=out_rows[image, channels, first : first + GROUP], in_=y_sb[:])
 
         transpose_x(0)
         quantise_x(0)
         for g in range(GROUPS):
             stage1(g, 0)
+            if g > 0:
+                quantise_h(g - 1, 2)
             if g + 1 < GROUPS:
                 transpose_x(g + 1)
             stage1(g, 1)
             quantise_h(g, 0)
             if g + 1 < GROUPS:
                 quantise_x(g + 1)
+            if g > 0:
+                stage2(g - 1, 0)
             stage1(g, 2)
             quantise_h(g, 1)
-            if g == 0:
-                quantise_stage2_weights()
+            if g > 0:
+                stage2(g - 1, 1)
             else:
-                stage2(g - 1)
-            quantise_h(g, 2)
-        stage2(GROUPS - 1)
+                quantise_stage2_weights()
+        quantise_h(GROUPS - 1, 2)
+        stage2(GROUPS - 1, 0)
+        stage2(GROUPS - 1, 1)

@@ -47,9 +47,8 @@ def tile_skconv2d_pa_t_e_kernel(
         pair = ctx.enter_context(tc.tile_pool(name="pair", bufs=2))
         hg_pool = ctx.enter_context(tc.tile_pool(name="h_grouped", bufs=3))
         y_pool = ctx.enter_context(tc.tile_pool(name="y", bufs=4))
-        xt_psum = ctx.enter_context(tc.psum_pool(name="xt_psum", bufs=2))
-        h_psum = ctx.enter_context(tc.psum_pool(name="h_psum", bufs=4))
-        y_psum = ctx.enter_context(tc.psum_pool(name="y_psum", bufs=2))
+        h_psum = ctx.enter_context(tc.psum_pool(name="h_psum", bufs=6))
+        side_psum = ctx.enter_context(tc.psum_pool(name="side_psum", bufs=2))
         ctx.enter_context(tc.manual_schedule())
 
         ident = const.tile([P, P], F32)
@@ -76,10 +75,6 @@ def tile_skconv2d_pa_t_e_kernel(
 
         def load_stage1_weights(words, scales, first, count):
             cols = slice(first, first + count)
-            nc.sync.dma_start(
-                out=w1_words[:, cols].bitcast(I32).rearrange("p (g n) -> p g n", g=TERMS),
-                in_=words.rearrange("g p n t -> p g (n t)").bitcast(I32),
-            )
             for quadrant in range(QUADRANTS):
                 nc.sync.dma_start(
                     out=w1_scales[32 * quadrant : 32 * quadrant + SCALE_ROWS, cols]
@@ -89,6 +84,10 @@ def tile_skconv2d_pa_t_e_kernel(
                     .rearrange("g r n -> r g n")
                     .bitcast(I32),
                 )
+            nc.sync.dma_start(
+                out=w1_words[:, cols].bitcast(I32).rearrange("p (g n) -> p g n", g=TERMS),
+                in_=words.rearrange("g p n t -> p g (n t)").bitcast(I32),
+            )
 
         w2_raw = const.tile([P, HIDDEN // P, OUT_CH], BF16)
 
@@ -139,7 +138,7 @@ def tile_skconv2d_pa_t_e_kernel(
             grouped = pair.tile([P, GROUP * PACK], BF16, align_bytes=64, name="x_grouped")
             grouped_words = grouped[:].bitcast(F32).rearrange("p (w u) -> p w u", u=2)
             for half in range(HALVES):
-                xt = xt_psum.tile([P, 2, HALF], F32, name="xt")
+                xt = side_psum.tile([P, 2, HALF], F32, name="xt", tag="side")
                 for s in range(HALF // P):
                     words = x_rows[(g, half)][:, s, :].bitcast(F32)
                     for u in range(2):
@@ -203,7 +202,7 @@ def tile_skconv2d_pa_t_e_kernel(
             image = GROUP * g // IMAGE
             first = GROUP * g % IMAGE
             channels = slice(P * t, P * (t + 1))
-            y_bank = y_psum.tile([P, GROUP], F32, name="y_bank")
+            y_bank = side_psum.tile([P, GROUP], F32, name="y_bank", tag="side")
             for c in range(HIDDEN_PASSES):
                 nc.tensor.matmul_mx(
                     out=y_bank[:],

@@ -75,6 +75,10 @@ def tile_skconv2d_pa_t_e_kernel(
 
         def load_stage1_weights(words, scales, first, count):
             cols = slice(first, first + count)
+            nc.sync.dma_start(
+                out=w1_words[:, cols].bitcast(I32).rearrange("p (g n) -> p g n", g=TERMS),
+                in_=words.rearrange("g p n t -> p g (n t)").bitcast(I32),
+            )
             for quadrant in range(QUADRANTS):
                 nc.sync.dma_start(
                     out=w1_scales[32 * quadrant : 32 * quadrant + SCALE_ROWS, cols]
@@ -84,10 +88,6 @@ def tile_skconv2d_pa_t_e_kernel(
                     .rearrange("g r n -> r g n")
                     .bitcast(I32),
                 )
-            nc.sync.dma_start(
-                out=w1_words[:, cols].bitcast(I32).rearrange("p (g n) -> p g n", g=TERMS),
-                in_=words.rearrange("g p n t -> p g (n t)").bitcast(I32),
-            )
 
         w2_raw = const.tile([P, HIDDEN // P, OUT_CH], BF16)
 

from contextlib import ExitStack

import concourse.mybir as mybir
from concourse.masks import make_identity

F32 = mybir.dt.float32
BF16 = mybir.dt.bfloat16
I32 = mybir.dt.int32
U32 = mybir.dt.uint32
U8 = mybir.dt.uint8
FP8X4 = mybir.dt.float8_e4m3fn_x4
IDENTITY = mybir.ActivationFunctionType.Identity

P = 128
PACK = 4
K_PASS = P * PACK

WINDOWS = 4096
D = 512
TERMS = 8
H1 = 512
HIDDEN = 1536
HIDDEN_PASSES = HIDDEN // K_PASS
OUT_CH = 256
OUT_TILES = OUT_CH // P
IMAGE = 1024

GROUP = 512
GROUPS = WINDOWS // GROUP
PIECE = 128
PIECES = GROUP // PIECE
HALVES = 2
HALF = GROUP // HALVES
SCALE_ROWS = 4
QUADRANTS = 4

FLOPS = 2 * WINDOWS * D * HIDDEN + 2 * WINDOWS * HIDDEN * OUT_CH


def tile_skconv2d_pa_t_e_kernel(
    tc, xw, S1s_words, S1s_scales, U1s, U2s_words, U2s_scales, S2s, bias, out
):
    nc = tc.nc
    with ExitStack() as ctx:
        const = ctx.enter_context(tc.tile_pool(name="const", bufs=1))
        x_pool = ctx.enter_context(tc.tile_pool(name="x_rows", bufs=GROUPS * HALVES))
        pair = ctx.enter_context(tc.tile_pool(name="pair", bufs=2))
        hg_pool = ctx.enter_context(tc.tile_pool(name="h_grouped", bufs=3))
        y_pool = ctx.enter_context(tc.tile_pool(name="y", bufs=4))
        h_psum = ctx.enter_context(tc.psum_pool(name="h_psum", bufs=6))
        side_psum = ctx.enter_context(tc.psum_pool(name="side_psum", bufs=2))
        ctx.enter_context(tc.manual_schedule())

        ident = const.tile([P, P], F32)
        make_identity(nc, ident[:])

        w1_words = const.tile([P, HIDDEN], U32, align_bytes=64)
        w1_scales = const.tile([P, HIDDEN], U8, align_bytes=64)
        nc.vector.memset(w1_scales[:].bitcast(I32), 0)

        bias_cols = const.tile([P, OUT_TILES], BF16)
        with nc.allow_non_contiguous_dma(reason="256 bias values, one per partition and tile"):
            nc.sync.dma_start(out=bias_cols[:], in_=bias.rearrange("(t p) -> p t", p=P))

        x_rows = {}

        def load_x(g):
            for half in range(HALVES):
                first = GROUP * g + HALF * half
                rows = x_pool.tile([P, HALF // P, D], BF16, name="x_rows")
                nc.sync.dma_start(
                    out=rows[:], in_=xw[first : first + HALF, :].rearrange("(s p) d -> p s d", p=P)
                )
                x_rows[(g, half)] = rows

        def load_stage1_weights(words, scales, first, count):
            cols = slice(first, first + count)
            nc.sync.dma_start(
                out=w1_words[:, cols].bitcast(I32).rearrange("p (g n) -> p g n", g=TERMS),
                in_=words.rearrange("g p n t -> p g (n t)").bitcast(I32),
            )
            for quadrant in range(QUADRANTS):
                nc.sync.dma_start(
                    out=w1_scales[32 * quadrant : 32 * quadrant + SCALE_ROWS, cols]
                    .bitcast(I32)
                    .rearrange("r (g n) -> r g n", g=TERMS),
                    in_=scales[:, SCALE_ROWS * quadrant : SCALE_ROWS * (quadrant + 1), :]
                    .rearrange("g r n -> r g n")
                    .bitcast(I32),
                )

        w2_raw = const.tile([P, HIDDEN // P, OUT_CH], BF16)

        load_x(0)
        load_stage1_weights(S1s_words, S1s_scales, 0, H1)
        load_x(1)
        load_stage1_weights(U2s_words, U2s_scales, H1, HIDDEN - H1)
        nc.sync.dma_start(
            out=w2_raw[:, 0 : H1 // P, :],
            in_=U1s.rearrange("t r o -> (t r) o").rearrange("(m p) o -> p m o", p=P),
        )
        nc.sync.dma_start(
            out=w2_raw[:, H1 // P :, :],
            in_=S2s.rearrange("t r o -> (t r) o").rearrange("(m p) o -> p m o", p=P),
        )
        for g in range(2, GROUPS):
            load_x(g)

        bias2 = const.tile([P, OUT_TILES], F32)
        nc.scalar.activation(out=bias2[:], in_=bias_cols[:], func=IDENTITY, scale=2.0)

        w2_grouped = const.tile([P, HIDDEN_PASSES, OUT_CH, PACK], BF16, align_bytes=64)
        w2_words = const.tile([P, HIDDEN_PASSES, OUT_CH], U32, align_bytes=64)
        w2_scales = const.tile([P, HIDDEN_PASSES, OUT_CH], U8, align_bytes=64)

        def quantise_stage2_weights():
            for c in range(HIDDEN_PASSES):
                copy = nc.scalar.copy if c < HIDDEN_PASSES - 1 else nc.vector.tensor_copy
                copy(
                    out=w2_grouped[:, c],
                    in_=w2_raw[:, PACK * c : PACK * (c + 1), :].rearrange("p j o -> p o j"),
                )
            for c in range(HIDDEN_PASSES):
                nc.vector.quantize_mx(
                    out=w2_words[:, c, :].bitcast(FP8X4),
                    scales=w2_scales[:, c, :],
                    in_=w2_grouped[:, c].rearrange("p o j -> p (o j)"),
                )

        x_grouped = {}
        x_words = {}
        x_scales = {}
        h_grouped = {}
        h_words = {}
        h_scales = {}

        def transpose_x(g):
            grouped = pair.tile([P, GROUP * PACK], BF16, align_bytes=64, name="x_grouped")
            grouped_words = grouped[:].bitcast(F32).rearrange("p (w u) -> p w u", u=2)
            for half in range(HALVES):
                xt = side_psum.tile([P, 2, HALF], F32, name="xt", tag="side")
                for s in range(HALF // P):
                    words = x_rows[(g, half)][:, s, :].bitcast(F32)
                    for u in range(2):
                        nc.tensor.transpose(
                            xt[:, u, P * s : P * (s + 1)], words[:, u : D // 2 : 2], ident[:]
                        )
                nc.scalar.copy(
                    out=grouped_words[:, HALF * half : HALF * (half + 1), :],
                    in_=xt[:].rearrange("p u w -> p w u"),
                )
            x_grouped[g] = grouped

        def quantise_x(g):
            words = pair.tile([P, GROUP], U32, align_bytes=64, name="x_words")
            scales = pair.tile([P, GROUP], U8, align_bytes=64, name="x_scales")
            for half in range(HALVES):
                windows = slice(HALF * half, HALF * (half + 1))
                nc.vector.quantize_mx(
                    out=words[:, windows].bitcast(FP8X4),
                    scales=scales[:, windows],
                    in_=x_grouped[g][:, PACK * HALF * half : PACK * HALF * (half + 1)],
                )
            x_words[g] = words
            x_scales[g] = scales

        def stage1(g, c):
            grouped = hg_pool.tile([P, GROUP, PACK], BF16, align_bytes=64, name="h_grouped")
            for q in range(PIECES):
                windows = slice(PIECE * q, PIECE * (q + 1))
                h_bank = h_psum.tile([P, PACK, PIECE], F32, name="h_bank")
                for j in range(PACK):
                    rows = slice(K_PASS * c + P * j, K_PASS * c + P * (j + 1))
                    nc.tensor.matmul_mx(
                        out=h_bank[:, j, :],
                        lhsT=w1_words[:, rows].bitcast(FP8X4),
                        lhsT_scale=w1_scales[:, rows],
                        rhs=x_words[g][:, windows].bitcast(FP8X4),
                        rhs_scale=x_scales[g][:, windows],
                        start=True,
                        stop=True,
                    )
                copy = nc.scalar.copy if q % 2 == 0 else nc.vector.tensor_copy
                copy(out=grouped[:, windows, :], in_=h_bank[:].rearrange("p j w -> p w j"))
            h_grouped[(g, c)] = grouped

        def quantise_h(g, c):
            if c == 0:
                words = pair.tile([P, HIDDEN_PASSES, GROUP], U32, align_bytes=64, name="h_words")
                scales = pair.tile([P, HIDDEN_PASSES, GROUP], U8, align_bytes=64, name="h_scales")
                h_words[g] = words
                h_scales[g] = scales
            nc.vector.quantize_mx(
                out=h_words[g][:, c, :].bitcast(FP8X4),
                scales=h_scales[g][:, c, :],
                in_=h_grouped[(g, c)][:].rearrange("p w j -> p (w j)"),
            )

        out_rows = out.rearrange("b o i j -> b o (i j)")

        def stage2(g, t):
            image = GROUP * g // IMAGE
            first = GROUP * g % IMAGE
            channels = slice(P * t, P * (t + 1))
            y_bank = side_psum.tile([P, GROUP], F32, name="y_bank", tag="side")
            for c in range(HIDDEN_PASSES):
                nc.tensor.matmul_mx(
                    out=y_bank[:],
                    lhsT=w2_words[:, c, channels].bitcast(FP8X4),
                    lhsT_scale=w2_scales[:, c, channels],
                    rhs=h_words[g][:, c, :].bitcast(FP8X4),
                    rhs_scale=h_scales[g][:, c, :],
                    start=(c == 0),
                    stop=(c == HIDDEN_PASSES - 1),
                )
            y_sb = y_pool.tile([P, GROUP], F32, name="y_sb")
            nc.scalar.activation(
                out=y_sb[:], in_=y_bank[:], func=IDENTITY, bias=bias2[:, t : t + 1], scale=1.0 / TERMS
            )
            nc.sync.dma_start(out=out_rows[image, channels, first : first + GROUP], in_=y_sb[:])

        transpose_x(0)
        quantise_x(0)
        for g in range(GROUPS):
            stage1(g, 0)
            if g > 0:
                quantise_h(g - 1, 2)
            if g + 1 < GROUPS:
                transpose_x(g + 1)
            stage1(g, 1)
            quantise_h(g, 0)
            if g + 1 < GROUPS:
                quantise_x(g + 1)
            if g > 0:
                stage2(g - 1, 0)
            stage1(g, 2)
            quantise_h(g, 1)
            if g > 0:
                stage2(g - 1, 1)
            else:
                quantise_stage2_weights()
        quantise_h(GROUPS - 1, 2)
        stage2(GROUPS - 1, 0)
        stage2(GROUPS - 1, 1)
